import numpy as np
import ml_dtypes


def mxq(x, axis, fmt="e4m3"):
    dtype, down = {"e4m3": (ml_dtypes.float8_e4m3fn, 7), "e5m2": (ml_dtypes.float8_e5m2, 14)}[fmt]
    v = np.moveaxis(np.asarray(x, np.float32).astype(ml_dtypes.bfloat16).astype(np.float64), axis, -1)
    blocks = v.reshape(v.shape[:-1] + (-1, 32))
    amax = np.abs(blocks).max(-1, keepdims=True)
    byte = np.maximum(np.where(amax > 0, np.frexp(amax)[1] - 1 + 127, 0) - down, 1)
    scale = np.exp2(byte - 127.0)
    codes = (blocks / scale).astype(np.float32).astype(dtype).astype(np.float64)
    return np.moveaxis((codes * scale).reshape(v.shape), -1, axis)


WIDE = False


def mx_kscale(k):
    if not WIDE:
        return np.ones(k)
    levels = np.array([10, -10, 5, -5, 0])
    a = np.random.permutation(np.resize(levels, k // 512 * 4)).reshape(k // 512, 4)
    idx = np.arange(k)
    return np.exp2(a[idx // 512, idx % 128 // 32])


BF16 = ml_dtypes.bfloat16


def bf(x):
    return np.asarray(x, np.float32).astype(BF16)


def f64(x):
    return np.asarray(x).astype(np.float64)


B, C, NP, P, HID = 32, 3, 8, 32, 512
IN_D = C * P * P
SEQ = NP * NP + 1
IMG = NP * P


def positional_embedding(seq_len, dim):
    i = np.arange(seq_len)[:, None].astype(np.float64)
    j = np.arange(dim)[None, :].astype(np.float64)
    ang = i / np.power(100000.0, j / dim)
    return np.where(j % 2 == 0, np.sin(ang), np.cos(ang))


def setup_inputs():
    s = mx_kscale(IN_D)
    X = np.random.standard_normal((B, C, NP, P, NP, P)) * s.reshape(1, C, 1, P, 1, P)
    bound = 2.0 / np.sqrt(IN_D)
    return {"X": bf(X.reshape(B, C, IMG, IMG)),
            "W": bf(np.random.uniform(-bound, bound, (HID, IN_D)) / s[None, :]),
            "b": bf(np.random.standard_normal(HID) * 0.3),
            "class_token": bf(np.random.uniform(0.0, 1.0, (1, HID))),
            "pos_embed": bf(positional_embedding(SEQ, HID))}


def reference(X, W, b, class_token, pos_embed):
    nb = X.shape[0]
    patches = f64(X).reshape(nb, C, NP, P, NP, P)
    patches = patches.transpose(0, 2, 4, 1, 3, 5).reshape(nb, NP * NP, IN_D)
    tokens = (mxq(patches, 2, "e4m3") @ mxq(f64(W), 1, "e4m3").T) + f64(b)
    cls = np.broadcast_to(f64(class_token)[None, :, :], (nb, 1, HID))
    tokens = np.concatenate([cls, tokens], axis=1)
    return tokens * f64(pos_embed)[None, :, :]

@@ -1,0 +1,221 @@
+from contextlib import ExitStack
+
+import concourse.mybir as mybir
+from concourse.masks import make_identity
+
+F32 = mybir.dt.float32
+BF16 = mybir.dt.bfloat16
+U32 = mybir.dt.uint32
+U8 = mybir.dt.uint8
+FP8X4 = mybir.dt.float8_e4m3fn_x4
+ADD = mybir.AluOpType.add
+MULT = mybir.AluOpType.mult
+
+P = 128
+HID = 512
+NG = 6
+NCHUNK = 12
+FLOPS = 2 * 2048 * 3072 * 512
+
+
+def tile_myvit_kernel(tc, X, W, b, class_token, pos_embed, out):
+    nc = tc.nc
+    with ExitStack() as ctx:
+        ctx.enter_context(tc.manual_schedule())
+        keep = ctx.enter_context(tc.tile_pool(name="keep", bufs=1))
+        rawp = ctx.enter_context(tc.tile_pool(name="rawp", bufs=5))
+        work = ctx.enter_context(tc.tile_pool(name="work", bufs=2))
+        outp = ctx.enter_context(tc.tile_pool(name="outp", bufs=4))
+        psum = ctx.enter_context(tc.psum_pool(name="psum", bufs=1))
+
+        ident = keep.tile([P, P], F32, name="ident")
+        make_identity(nc, ident[:])
+        bias = keep.tile([P, HID], BF16, name="bias")
+        nc.scalar.dma_start(out=bias[:], in_=b.partition_broadcast(P))
+        ct = keep.tile([32, HID], BF16, name="ct")
+        nc.scalar.dma_start(out=ct[:], in_=class_token.broadcast_to([32, HID]))
+        p0 = keep.tile([32, HID], BF16, name="p0")
+        nc.scalar.dma_start(out=p0[:], in_=pos_embed[0:1, :].broadcast_to([32, HID]))
+        cls = keep.tile([32, HID], F32, name="cls")
+        nc.gpsimd.tensor_tensor(out=cls[:], in0=ct[:], in1=p0[:], op=MULT)
+
+        wraw = keep.tile([P, 4, 3072], BF16, name="wraw")
+        w_view = W.rearrange("(t p) k -> p t k", p=P)
+        posq = keep.tile([P, 2, 8 * HID], BF16, name="posq")
+        pos_view = pos_embed[1:65, :].rearrange("(t l g) h -> l t (g h)", t=2, l=4, g=8)
+
+        xc = [keep.tile([P, 1024], U32, name="xc%d" % s, align_bytes=64) for s in range(NCHUNK)]
+        xs = [keep.tile([P, 1024], U8, name="xs%d" % s, align_bytes=64) for s in range(NCHUNK)]
+        wc = [keep.tile([P, HID], U32, name="wc%d" % g, align_bytes=64) for g in range(NG)]
+        ws = [keep.tile([P, HID], U8, name="ws%d" % g, align_bytes=64) for g in range(NG)]
+
+        raws = {}
+        rgs = {}
+
+        def load_w(i):
+            nc.sync.dma_start(out=wraw[:, :, i * 1024:(i + 1) * 1024], in_=w_view[:, :, i * 1024:(i + 1) * 1024])
+
+        def load_x(s):
+            qt, g = divmod(s, NG)
+            c, a = divmod(g, 2)
+            raw = rawp.tile([P, 4096], BF16, name="raw%d" % s, tag="raw")
+            for l in range(4):
+                y0 = (qt * 4 + l) * 32 + a * 16
+                nc.sync.dma_start(out=raw[l:P:4, :], in_=X[:, c, y0:y0 + 16, :].rearrange("b y x -> b (y x)"))
+            raws[s] = raw
+
+        def load_pos(qt):
+            for l in range(4):
+                nc.sync.dma_start(out=posq[l:P:4, qt, :], in_=pos_view[l, qt:qt + 1, :].broadcast_to([32, 8 * HID]))
+
+        def regroup(s):
+            rg = work.tile([P, 4096], BF16, name="rg%d" % s, tag="rg")
+            nc.vector.tensor_copy(
+                out=rg[:].rearrange("p (g y x) -> p g y x", g=8, x=32),
+                in_=raws[s][:].rearrange("p (y g x) -> p g y x", g=8, x=32),
+            )
+            rgs[s] = rg
+
+        state = {"tb": 0, "ep": 0}
+
+        def t_bank(banks):
+            i = banks[state["tb"] % len(banks)]
+            state["tb"] += 1
+            return psum.tile([P, 4, P], F32, name="tp%d" % state["tb"], tag="bk%d" % i)
+
+        wgrs = {}
+
+        def transpose_w(g, banks):
+            wgr = work.tile([P, 2048], BF16, name="wgr%d" % g, tag="wgr", align_bytes=64)
+            wgrf = wgr[:].bitcast(F32).rearrange("p (t h u) -> p t h u", t=4, u=2)
+            for j in range(2):
+                bank = t_bank(banks)
+                for tl in range(2):
+                    src = wraw[:, 2 * j + tl, :].bitcast(F32)
+                    for u in range(2):
+                        k0 = g * 256 + u * 128
+                        nc.tensor.transpose(out=bank[:, 2 * tl + u, :], in_=src[:, k0:k0 + 128], identity=ident[:])
+                nc.scalar.copy(out=wgrf[:, 2 * j:2 * j + 2, :, :], in_=bank[:].rearrange("p (t u) h -> p t h u", u=2))
+            wgrs[g] = wgr
+
+        grs = {}
+
+        def transpose_x(s, hf, banks):
+            if hf == 0:
+                grs[s] = work.tile([P, 4096], BF16, name="gr%d" % s, tag="gr", align_bytes=64)
+            grf = grs[s][:].bitcast(F32).rearrange("p (g q u) -> p g q u", g=8, u=2)
+            rgf = rgs[s][:].bitcast(F32)
+            for j in range(2):
+                bank = t_bank(banks)
+                g0 = 4 * hf + 2 * j
+                for gl in range(2):
+                    for u in range(2):
+                        k0 = (g0 + gl) * 256 + u * 128
+                        nc.tensor.transpose(out=bank[:, 2 * gl + u, :], in_=rgf[:, k0:k0 + 128], identity=ident[:])
+                nc.scalar.copy(out=grf[:, g0:g0 + 2, :, :], in_=bank[:].rearrange("p (g u) q -> p g q u", u=2))
+
+        def quant_w(g):
+            nc.vector.quantize_mx(out=wc[g][:].bitcast(FP8X4), scales=ws[g][:], in_=wgrs[g][:])
+
+        def quant_x(s, hf):
+            nc.vector.quantize_mx(
+                out=xc[s][:, hf * 512:(hf + 1) * 512].bitcast(FP8X4),
+                scales=xs[s][:, hf * 512:(hf + 1) * 512],
+                in_=grs[s][:, hf * 2048:(hf + 1) * 2048],
+            )
+
+        accs = {}
+        closed = []
+
+        def mx_pass(qt, gx, g, bank):
+            if g == 0:
+                accs[(qt, gx)] = psum.tile([P, HID], F32, name="acc%d_%d" % (qt, gx), tag="bk%d" % bank)
+            s = qt * NG + g
+            nc.tensor.matmul_mx(
+                out=accs[(qt, gx)][:],
+                lhsT=xc[s][:, gx * P:(gx + 1) * P].bitcast(FP8X4),
+                lhsT_scale=xs[s][:, gx * P:(gx + 1) * P],
+                rhs=wc[g][:].bitcast(FP8X4),
+                rhs_scale=ws[g][:],
+                start=(g == 0),
+                stop=(g == NG - 1),
+            )
+            if g == NG - 1:
+                closed.append((qt, gx))
+
+        osts = {}
+
+        def epilogue(qt, gx):
+            if gx % 2 == 0:
+                osts[(qt, gx // 2)] = outp.tile([P, 2, HID], F32, name="ost%d_%d" % (qt, gx // 2), tag="ost")
+            ost = osts[(qt, gx // 2)]
+            tmp = work.tile([P, HID], F32, name="tmp%d_%d" % (qt, gx), tag="tmp")
+            nc.vector.tensor_tensor(out=tmp[:], in0=accs[(qt, gx)][:], in1=bias[:], op=ADD)
+            nc.vector.tensor_tensor(out=ost[:, gx % 2, :], in0=tmp[:], in1=posq[:, qt, gx * HID:(gx + 1) * HID], op=MULT)
+            if gx % 2 == 1:
+                for l in range(4):
+                    r0 = 1 + (qt * 4 + l) * 8 + gx - 1
+                    nc.sync.dma_start(
+                        out=out[:, r0:r0 + 2, :].rearrange("b g h -> b (g h)"),
+                        in_=ost[l:P:4, :, :].rearrange("p g h -> p (g h)"),
+                    )
+
+        def flush_epilogues():
+            for qt, gx in closed[state["ep"]:]:
+                epilogue(qt, gx)
+            state["ep"] = len(closed)
+
+        load_w(0)
+        load_x(0)
+        load_x(1)
+        load_w(1)
+        load_x(2)
+        load_x(3)
+        load_w(2)
+        load_x(4)
+        regroup(0)
+
+        late0 = [(0, gx, g, 4 + gx % 2) for gx in range(4, 8) for g in range(NG)]
+        late1 = [(1, gx, g, gx) for gx in range(4, 8) for g in range(NG)]
+
+        def early(s):
+            qt, g = divmod(s, NG)
+            for gx in range(4):
+                mx_pass(qt, gx, g, gx)
+
+        for t in range(NCHUNK):
+            if t < NG:
+                banks = [4, 5, 6, 7]
+                transpose_w(t, banks)
+                transpose_x(t, 0, banks)
+                if t >= 1:
+                    early(t - 1)
+                transpose_x(t, 1, banks)
+            else:
+                banks = [6, 7]
+                transpose_x(t, 0, banks)
+                for item in late0[4 * (t - NG):4 * (t - NG) + 4]:
+                    mx_pass(*item)
+                transpose_x(t, 1, banks)
+                early(t - 1)
+            if t + 1 < NCHUNK:
+                regroup(t + 1)
+            if t + 5 < NCHUNK:
+                load_x(t + 5)
+            if t == 2:
+                load_pos(0)
+            if t == 6:
+                load_pos(1)
+            if t < NG:
+                quant_w(t)
+            quant_x(t, 0)
+            quant_x(t, 1)
+            flush_epilogues()
+
+        nc.sync.dma_start(out=out[:, 0, :], in_=cls[:])
+        early(NCHUNK - 1)
+        flush_epilogues()
+        for gx in range(4, 8):
+            for item in late1[NG * (gx - 4):NG * (gx - 3)]:
+                mx_pass(*item)
+            flush_epilogues()

@@ -39,7 +39,7 @@ def tile_myvit_kernel(tc, X, W, b, class_token, pos_embed, out):
         cls = keep.tile([32, HID], F32, name="cls")
         nc.gpsimd.tensor_tensor(out=cls[:], in0=ct[:], in1=p0[:], op=MULT)
 
-        wraw = keep.tile([P, 4, 3072], BF16, name="wraw")
+        wraw = [keep.tile([P, 4, 1024], BF16, name="wraw%d" % i) for i in range(3)]
         w_view = W.rearrange("(t p) k -> p t k", p=P)
         posq = keep.tile([P, 2, 8 * HID], BF16, name="posq")
         pos_view = pos_embed[1:65, :].rearrange("(t l g) h -> l t (g h)", t=2, l=4, g=8)
@@ -53,7 +53,7 @@ def tile_myvit_kernel(tc, X, W, b, class_token, pos_embed, out):
         rgs = {}
 
         def load_w(i):
-            nc.sync.dma_start(out=wraw[:, :, i * 1024:(i + 1) * 1024], in_=w_view[:, :, i * 1024:(i + 1) * 1024])
+            nc.sync.dma_start(out=wraw[i][:], in_=w_view[:, :, i * 1024:(i + 1) * 1024])
 
         def load_x(s):
             qt, g = divmod(s, NG)
@@ -91,9 +91,9 @@ def tile_myvit_kernel(tc, X, W, b, class_token, pos_embed, out):
             for j in range(2):
                 bank = t_bank(banks)
                 for tl in range(2):
-                    src = wraw[:, 2 * j + tl, :].bitcast(F32)
+                    src = wraw[g // 2][:, 2 * j + tl, :].bitcast(F32)
                     for u in range(2):
-                        k0 = g * 256 + u * 128
+                        k0 = (g % 2) * 256 + u * 128
                         nc.tensor.transpose(out=bank[:, 2 * tl + u, :], in_=src[:, k0:k0 + 128], identity=ident[:])
                 nc.scalar.copy(out=wgrf[:, 2 * j:2 * j + 2, :, :], in_=bank[:].rearrange("p (t u) h -> p t h u", u=2))
             wgrs[g] = wgr

@@ -41,7 +41,7 @@ def tile_myvit_kernel(tc, X, W, b, class_token, pos_embed, out):
 
         wraw = [keep.tile([P, 4, 1024], BF16, name="wraw%d" % i) for i in range(3)]
         w_view = W.rearrange("(t p) k -> p t k", p=P)
-        posq = keep.tile([P, 2, 8 * HID], BF16, name="posq")
+        posq = [keep.tile([P, 8 * HID], BF16, name="posq%d" % qt) for qt in range(2)]
         pos_view = pos_embed[1:65, :].rearrange("(t l g) h -> l t (g h)", t=2, l=4, g=8)
 
         xc = [keep.tile([P, 1024], U32, name="xc%d" % s, align_bytes=64) for s in range(NCHUNK)]
@@ -66,30 +66,37 @@ def tile_myvit_kernel(tc, X, W, b, class_token, pos_embed, out):
 
         def load_pos(qt):
             for l in range(4):
-                nc.sync.dma_start(out=posq[l:P:4, qt, :], in_=pos_view[l, qt:qt + 1, :].broadcast_to([32, 8 * HID]))
+                nc.sync.dma_start(out=posq[qt][l:P:4, :], in_=pos_view[l, qt:qt + 1, :].broadcast_to([32, 8 * HID]))
 
         def regroup(s):
+            nv = 8 if s < NG else 4
             rg = work.tile([P, 4096], BF16, name="rg%d" % s, tag="rg")
             nc.vector.tensor_copy(
-                out=rg[:].rearrange("p (g y x) -> p g y x", g=8, x=32),
-                in_=raws[s][:].rearrange("p (y g x) -> p g y x", g=8, x=32),
+                out=rg[:, 0:nv * 512].rearrange("p (g y x) -> p g y x", g=nv, x=32),
+                in_=raws[s][:].rearrange("p (y g x) -> p g y x", g=8, x=32)[:, 0:nv, :, :],
             )
+            if nv < 8:
+                nc.scalar.copy(
+                    out=rg[:].bitcast(F32).rearrange("p (g y w) -> p g y w", g=8, w=16)[:, nv:8, :, :],
+                    in_=raws[s][:].bitcast(F32).rearrange("p (y g w) -> p g y w", g=8, w=16)[:, nv:8, :, :],
+                )
             rgs[s] = rg
 
-        state = {"tb": 0, "ep": 0}
+        state = {"rot": 0, "n": 0, "e1": 0, "e2": 0}
 
-        def t_bank(banks):
-            i = banks[state["tb"] % len(banks)]
-            state["tb"] += 1
-            return psum.tile([P, 4, P], F32, name="tp%d" % state["tb"], tag="bk%d" % i)
+        def t_bank():
+            i = 4 + state["rot"]
+            state["rot"] = (state["rot"] + 1) % 4
+            state["n"] += 1
+            return psum.tile([P, 4, P], F32, name="tp%d" % state["n"], tag="bk%d" % i)
 
         wgrs = {}
 
-        def transpose_w(g, banks):
+        def transpose_w(g):
             wgr = work.tile([P, 2048], BF16, name="wgr%d" % g, tag="wgr", align_bytes=64)
             wgrf = wgr[:].bitcast(F32).rearrange("p (t h u) -> p t h u", t=4, u=2)
             for j in range(2):
-                bank = t_bank(banks)
+                bank = t_bank()
                 for tl in range(2):
                     src = wraw[g // 2][:, 2 * j + tl, :].bitcast(F32)
                     for u in range(2):
@@ -100,13 +107,13 @@ def tile_myvit_kernel(tc, X, W, b, class_token, pos_embed, out):
 
         grs = {}
 
-        def transpose_x(s, hf, banks):
+        def transpose_x(s, hf):
             if hf == 0:
                 grs[s] = work.tile([P, 4096], BF16, name="gr%d" % s, tag="gr", align_bytes=64)
             grf = grs[s][:].bitcast(F32).rearrange("p (g q u) -> p g q u", g=8, u=2)
             rgf = rgs[s][:].bitcast(F32)
             for j in range(2):
-                bank = t_bank(banks)
+                bank = t_bank()
                 g0 = 4 * hf + 2 * j
                 for gl in range(2):
                     for u in range(2):
@@ -144,59 +151,65 @@ def tile_myvit_kernel(tc, X, W, b, class_token, pos_embed, out):
                 closed.append((qt, gx))
 
         osts = {}
+        tmps = {}
 
-        def epilogue(qt, gx):
-            if gx % 2 == 0:
-                osts[(qt, gx // 2)] = outp.tile([P, 2, HID], F32, name="ost%d_%d" % (qt, gx // 2), tag="ost")
-            ost = osts[(qt, gx // 2)]
-            tmp = work.tile([P, HID], F32, name="tmp%d_%d" % (qt, gx), tag="tmp")
-            nc.vector.tensor_tensor(out=tmp[:], in0=accs[(qt, gx)][:], in1=bias[:], op=ADD)
-            nc.vector.tensor_tensor(out=ost[:, gx % 2, :], in0=tmp[:], in1=posq[:, qt, gx * HID:(gx + 1) * HID], op=MULT)
-            if gx % 2 == 1:
-                for l in range(4):
-                    r0 = 1 + (qt * 4 + l) * 8 + gx - 1
-                    nc.sync.dma_start(
-                        out=out[:, r0:r0 + 2, :].rearrange("b g h -> b (g h)"),
-                        in_=ost[l:P:4, :, :].rearrange("p g h -> p (g h)"),
-                    )
+        def add_bias():
+            for qt, gx in closed[state["e1"]:]:
+                tmp = outp.tile([P, HID], F32, name="tmp%d_%d" % (qt, gx), tag="tmp", bufs=6)
+                nc.vector.tensor_tensor(out=tmp[:], in0=accs[(qt, gx)][:], in1=bias[:], op=ADD)
+                tmps[(qt, gx)] = tmp
+            state["e1"] = len(closed)
 
-        def flush_epilogues():
-            for qt, gx in closed[state["ep"]:]:
-                epilogue(qt, gx)
-            state["ep"] = len(closed)
-
-        load_w(0)
-        load_x(0)
-        load_x(1)
-        load_w(1)
-        load_x(2)
-        load_x(3)
-        load_w(2)
-        load_x(4)
-        regroup(0)
-
-        late0 = [(0, gx, g, 4 + gx % 2) for gx in range(4, 8) for g in range(NG)]
-        late1 = [(1, gx, g, gx) for gx in range(4, 8) for g in range(NG)]
+        def times_pos():
+            for qt, gx in closed[state["e2"]:]:
+                if gx % 2 == 0:
+                    osts[(qt, gx // 2)] = outp.tile([P, 2, HID], F32, name="ost%d_%d" % (qt, gx // 2), tag="ost")
+                ost = osts[(qt, gx // 2)]
+                on_pool = (qt == 0 and gx < 4) or (qt == 1 and gx % 2 == 0)
+                eng = nc.gpsimd if on_pool else nc.vector
+                eng.tensor_tensor(out=ost[:, gx % 2, :], in0=tmps[(qt, gx)][:], in1=posq[qt][:, gx * HID:(gx + 1) * HID], op=MULT)
+                if gx % 2 == 1:
+                    for l in range(4):
+                        r0 = 1 + (qt * 4 + l) * 8 + gx - 1
+                        nc.sync.dma_start(
+                            out=out[:, r0:r0 + 2, :].rearrange("b g h -> b (g h)"),
+                            in_=ost[l:P:4, :, :].rearrange("p g h -> p (g h)"),
+                        )
+            state["e2"] = len(closed)
 
         def early(s):
             qt, g = divmod(s, NG)
             for gx in range(4):
                 mx_pass(qt, gx, g, gx)
 
+        def whole_group(qt, gx, bank):
+            for g in range(NG):
+                mx_pass(qt, gx, g, bank)
+
+        load_x(0)
+        load_w(0)
+        load_x(1)
+        load_x(2)
+        load_w(1)
+        load_x(3)
+        load_x(4)
+        load_w(2)
+        regroup(0)
+
         for t in range(NCHUNK):
             if t < NG:
-                banks = [4, 5, 6, 7]
-                transpose_w(t, banks)
-                transpose_x(t, 0, banks)
+                transpose_x(t, 0)
+                transpose_w(t)
                 if t >= 1:
                     early(t - 1)
-                transpose_x(t, 1, banks)
+                transpose_x(t, 1)
             else:
-                banks = [6, 7]
-                transpose_x(t, 0, banks)
-                for item in late0[4 * (t - NG):4 * (t - NG) + 4]:
-                    mx_pass(*item)
-                transpose_x(t, 1, banks)
+                first = 4 + state["rot"]
+                transpose_x(t, 0)
+                transpose_x(t, 1)
+                if t < NG + 4:
+                    whole_group(0, t - 2, first)
+                    state["rot"] = (state["rot"] + 1) % 4
                 early(t - 1)
             if t + 1 < NCHUNK:
                 regroup(t + 1)
@@ -210,12 +223,14 @@ def tile_myvit_kernel(tc, X, W, b, class_token, pos_embed, out):
                 quant_w(t)
             quant_x(t, 0)
             quant_x(t, 1)
-            flush_epilogues()
+            add_bias()
+            times_pos()
 
         nc.sync.dma_start(out=out[:, 0, :], in_=cls[:])
         early(NCHUNK - 1)
-        flush_epilogues()
-        for gx in range(4, 8):
-            for item in late1[NG * (gx - 4):NG * (gx - 3)]:
-                mx_pass(*item)
-            flush_epilogues()
+        add_bias()
+        times_pos()
+        for i in range(4):
+            whole_group(1, 4 + i, 4 + (state["rot"] + i) % 4)
+            add_bias()
+            times_pos()

@@ -69,7 +69,7 @@ def tile_myvit_kernel(tc, X, W, b, class_token, pos_embed, out):
                 nc.sync.dma_start(out=posq[qt][l:P:4, :], in_=pos_view[l, qt:qt + 1, :].broadcast_to([32, 8 * HID]))
 
         def regroup(s):
-            nv = 8 if s < NG else 4
+            nv = 8
             rg = work.tile([P, 4096], BF16, name="rg%d" % s, tag="rg")
             nc.vector.tensor_copy(
                 out=rg[:, 0:nv * 512].rearrange("p (g y x) -> p g y x", g=nv, x=32),
@@ -124,12 +124,8 @@ def tile_myvit_kernel(tc, X, W, b, class_token, pos_embed, out):
         def quant_w(g):
             nc.vector.quantize_mx(out=wc[g][:].bitcast(FP8X4), scales=ws[g][:], in_=wgrs[g][:])
 
-        def quant_x(s, hf):
-            nc.vector.quantize_mx(
-                out=xc[s][:, hf * 512:(hf + 1) * 512].bitcast(FP8X4),
-                scales=xs[s][:, hf * 512:(hf + 1) * 512],
-                in_=grs[s][:, hf * 2048:(hf + 1) * 2048],
-            )
+        def quant_x(s):
+            nc.vector.quantize_mx(out=xc[s][:].bitcast(FP8X4), scales=xs[s][:], in_=grs[s][:])
 
         accs = {}
         closed = []
@@ -165,7 +161,7 @@ def tile_myvit_kernel(tc, X, W, b, class_token, pos_embed, out):
                 if gx % 2 == 0:
                     osts[(qt, gx // 2)] = outp.tile([P, 2, HID], F32, name="ost%d_%d" % (qt, gx // 2), tag="ost")
                 ost = osts[(qt, gx // 2)]
-                on_pool = (qt == 0 and gx < 4) or (qt == 1 and gx % 2 == 0)
+                on_pool = qt == 0 or gx < 4 or gx % 2 == 0
                 eng = nc.gpsimd if on_pool else nc.vector
                 eng.tensor_tensor(out=ost[:, gx % 2, :], in0=tmps[(qt, gx)][:], in1=posq[qt][:, gx * HID:(gx + 1) * HID], op=MULT)
                 if gx % 2 == 1:
@@ -221,8 +217,7 @@ def tile_myvit_kernel(tc, X, W, b, class_token, pos_embed, out):
                 load_pos(1)
             if t < NG:
                 quant_w(t)
-            quant_x(t, 0)
-            quant_x(t, 1)
+            quant_x(t)
             add_bias()
             times_pos()
 

@@ -69,7 +69,7 @@ def tile_myvit_kernel(tc, X, W, b, class_token, pos_embed, out):
                 nc.sync.dma_start(out=posq[qt][l:P:4, :], in_=pos_view[l, qt:qt + 1, :].broadcast_to([32, 8 * HID]))
 
         def regroup(s):
-            nv = 8
+            nv = 8 if s < NG else 4
             rg = work.tile([P, 4096], BF16, name="rg%d" % s, tag="rg")
             nc.vector.tensor_copy(
                 out=rg[:, 0:nv * 512].rearrange("p (g y x) -> p g y x", g=nv, x=32),
@@ -124,8 +124,12 @@ def tile_myvit_kernel(tc, X, W, b, class_token, pos_embed, out):
         def quant_w(g):
             nc.vector.quantize_mx(out=wc[g][:].bitcast(FP8X4), scales=ws[g][:], in_=wgrs[g][:])
 
-        def quant_x(s):
-            nc.vector.quantize_mx(out=xc[s][:].bitcast(FP8X4), scales=xs[s][:], in_=grs[s][:])
+        def quant_x(s, hf):
+            nc.vector.quantize_mx(
+                out=xc[s][:, hf * 512:(hf + 1) * 512].bitcast(FP8X4),
+                scales=xs[s][:, hf * 512:(hf + 1) * 512],
+                in_=grs[s][:, hf * 2048:(hf + 1) * 2048],
+            )
 
         accs = {}
         closed = []
@@ -146,31 +150,40 @@ def tile_myvit_kernel(tc, X, W, b, class_token, pos_embed, out):
             if g == NG - 1:
                 closed.append((qt, gx))
 
-        osts = {}
         tmps = {}
 
         def add_bias():
             for qt, gx in closed[state["e1"]:]:
-                tmp = outp.tile([P, HID], F32, name="tmp%d_%d" % (qt, gx), tag="tmp", bufs=6)
-                nc.vector.tensor_tensor(out=tmp[:], in0=accs[(qt, gx)][:], in1=bias[:], op=ADD)
-                tmps[(qt, gx)] = tmp
+                if gx % 2 == 0:
+                    tmps[(qt, gx // 2)] = outp.tile([P, 2, HID], F32, name="tmp%d_%d" % (qt, gx // 2), tag="tmp")
+                nc.vector.tensor_tensor(out=tmps[(qt, gx // 2)][:, gx % 2, :], in0=accs[(qt, gx)][:], in1=bias[:], op=ADD)
             state["e1"] = len(closed)
+
+        def store(qt, gx, n, ost):
+            for l in range(4):
+                r0 = 1 + (qt * 4 + l) * 8 + gx
+                nc.sync.dma_start(
+                    out=out[:, r0:r0 + n, :].rearrange("b g h -> b (g h)"),
+                    in_=ost[l:P:4, :, :].rearrange("p g h -> p (g h)"),
+                )
 
         def times_pos():
             for qt, gx in closed[state["e2"]:]:
-                if gx % 2 == 0:
-                    osts[(qt, gx // 2)] = outp.tile([P, 2, HID], F32, name="ost%d_%d" % (qt, gx // 2), tag="ost")
-                ost = osts[(qt, gx // 2)]
-                on_pool = qt == 0 or gx < 4 or gx % 2 == 0
-                eng = nc.gpsimd if on_pool else nc.vector
-                eng.tensor_tensor(out=ost[:, gx % 2, :], in0=tmps[(qt, gx)][:], in1=posq[qt][:, gx * HID:(gx + 1) * HID], op=MULT)
-                if gx % 2 == 1:
-                    for l in range(4):
-                        r0 = 1 + (qt * 4 + l) * 8 + gx - 1
-                        nc.sync.dma_start(
-                            out=out[:, r0:r0 + 2, :].rearrange("b g h -> b (g h)"),
-                            in_=ost[l:P:4, :, :].rearrange("p g h -> p (g h)"),
-                        )
+                tmp = tmps[(qt, gx // 2)]
+                if (qt, gx // 2) == (1, 3):
+                    ost = outp.tile([P, 1, HID], F32, name="ostl%d" % gx, tag="ostl", bufs=2)
+                    nc.vector.tensor_tensor(out=ost[:, 0, :], in0=tmp[:, gx % 2, :], in1=posq[qt][:, gx * HID:(gx + 1) * HID], op=MULT)
+                    store(qt, gx, 1, ost)
+                elif gx % 2 == 1:
+                    ost = outp.tile([P, 2, HID], F32, name="ost%d_%d" % (qt, gx // 2), tag="ost", bufs=3)
+                    eng = nc.gpsimd if (qt, gx // 2) in ((1, 1), (1, 2)) else nc.vector
+                    eng.tensor_tensor(
+                        out=ost[:].rearrange("p g h -> p (g h)"),
+                        in0=tmp[:].rearrange("p g h -> p (g h)"),
+                        in1=posq[qt][:, (gx - 1) * HID:(gx + 1) * HID],
+                        op=MULT,
+                    )
+                    store(qt, gx - 1, 2, ost)
             state["e2"] = len(closed)
 
         def early(s):
@@ -217,7 +230,8 @@ def tile_myvit_kernel(tc, X, W, b, class_token, pos_embed, out):
                 load_pos(1)
             if t < NG:
                 quant_w(t)
-            quant_x(t)
+            quant_x(t, 0)
+            quant_x(t, 1)
             add_bias()
             times_pos()
 

@@ -72,8 +72,8 @@ def tile_myvit_kernel(tc, X, W, b, class_token, pos_embed, out):
             nv = 8 if s < NG else 4
             rg = work.tile([P, 4096], BF16, name="rg%d" % s, tag="rg")
             nc.vector.tensor_copy(
-                out=rg[:, 0:nv * 512].rearrange("p (g y x) -> p g y x", g=nv, x=32),
-                in_=raws[s][:].rearrange("p (y g x) -> p g y x", g=8, x=32)[:, 0:nv, :, :],
+                out=rg[:].bitcast(F32).rearrange("p (g y w) -> p g y w", g=8, w=16)[:, 0:nv, :, :],
+                in_=raws[s][:].bitcast(F32).rearrange("p (y g w) -> p g y w", g=8, w=16)[:, 0:nv, :, :],
             )
             if nv < 8:
                 nc.scalar.copy(
@@ -150,40 +150,31 @@ def tile_myvit_kernel(tc, X, W, b, class_token, pos_embed, out):
             if g == NG - 1:
                 closed.append((qt, gx))
 
+        osts = {}
         tmps = {}
 
         def add_bias():
             for qt, gx in closed[state["e1"]:]:
-                if gx % 2 == 0:
-                    tmps[(qt, gx // 2)] = outp.tile([P, 2, HID], F32, name="tmp%d_%d" % (qt, gx // 2), tag="tmp")
-                nc.vector.tensor_tensor(out=tmps[(qt, gx // 2)][:, gx % 2, :], in0=accs[(qt, gx)][:], in1=bias[:], op=ADD)
+                tmp = outp.tile([P, HID], F32, name="tmp%d_%d" % (qt, gx), tag="tmp", bufs=6)
+                nc.vector.tensor_tensor(out=tmp[:], in0=accs[(qt, gx)][:], in1=bias[:], op=ADD)
+                tmps[(qt, gx)] = tmp
             state["e1"] = len(closed)
-
-        def store(qt, gx, n, ost):
-            for l in range(4):
-                r0 = 1 + (qt * 4 + l) * 8 + gx
-                nc.sync.dma_start(
-                    out=out[:, r0:r0 + n, :].rearrange("b g h -> b (g h)"),
-                    in_=ost[l:P:4, :, :].rearrange("p g h -> p (g h)"),
-                )
 
         def times_pos():
             for qt, gx in closed[state["e2"]:]:
-                tmp = tmps[(qt, gx // 2)]
-                if (qt, gx // 2) == (1, 3):
-                    ost = outp.tile([P, 1, HID], F32, name="ostl%d" % gx, tag="ostl", bufs=2)
-                    nc.vector.tensor_tensor(out=ost[:, 0, :], in0=tmp[:, gx % 2, :], in1=posq[qt][:, gx * HID:(gx + 1) * HID], op=MULT)
-                    store(qt, gx, 1, ost)
-                elif gx % 2 == 1:
-                    ost = outp.tile([P, 2, HID], F32, name="ost%d_%d" % (qt, gx // 2), tag="ost", bufs=3)
-                    eng = nc.gpsimd if (qt, gx // 2) in ((1, 1), (1, 2)) else nc.vector
-                    eng.tensor_tensor(
-                        out=ost[:].rearrange("p g h -> p (g h)"),
-                        in0=tmp[:].rearrange("p g h -> p (g h)"),
-                        in1=posq[qt][:, (gx - 1) * HID:(gx + 1) * HID],
-                        op=MULT,
-                    )
-                    store(qt, gx - 1, 2, ost)
+                if gx % 2 == 0:
+                    osts[(qt, gx // 2)] = outp.tile([P, 2, HID], F32, name="ost%d_%d" % (qt, gx // 2), tag="ost")
+                ost = osts[(qt, gx // 2)]
+                on_pool = (qt == 0 and gx < 4) or (qt == 1 and gx % 2 == 0)
+                eng = nc.gpsimd if on_pool else nc.vector
+                eng.tensor_tensor(out=ost[:, gx % 2, :], in0=tmps[(qt, gx)][:], in1=posq[qt][:, gx * HID:(gx + 1) * HID], op=MULT)
+                if gx % 2 == 1:
+                    for l in range(4):
+                        r0 = 1 + (qt * 4 + l) * 8 + gx - 1
+                        nc.sync.dma_start(
+                            out=out[:, r0:r0 + 2, :].rearrange("b g h -> b (g h)"),
+                            in_=ost[l:P:4, :, :].rearrange("p g h -> p (g h)"),
+                        )
             state["e2"] = len(closed)
 
         def early(s):

from contextlib import ExitStack

import concourse.mybir as mybir
from concourse.masks import make_identity

F32 = mybir.dt.float32
BF16 = mybir.dt.bfloat16
U32 = mybir.dt.uint32
U8 = mybir.dt.uint8
FP8X4 = mybir.dt.float8_e4m3fn_x4
ADD = mybir.AluOpType.add
MULT = mybir.AluOpType.mult

P = 128
HID = 512
NG = 6
NCHUNK = 12
FLOPS = 2 * 2048 * 3072 * 512


def tile_myvit_kernel(tc, X, W, b, class_token, pos_embed, out):
    nc = tc.nc
    with ExitStack() as ctx:
        ctx.enter_context(tc.manual_schedule())
        keep = ctx.enter_context(tc.tile_pool(name="keep", bufs=1))
        rawp = ctx.enter_context(tc.tile_pool(name="rawp", bufs=5))
        work = ctx.enter_context(tc.tile_pool(name="work", bufs=2))
        outp = ctx.enter_context(tc.tile_pool(name="outp", bufs=4))
        psum = ctx.enter_context(tc.psum_pool(name="psum", bufs=1))

        ident = keep.tile([P, P], F32, name="ident")
        make_identity(nc, ident[:])
        bias = keep.tile([P, HID], BF16, name="bias")
        nc.scalar.dma_start(out=bias[:], in_=b.partition_broadcast(P))
        ct = keep.tile([32, HID], BF16, name="ct")
        nc.scalar.dma_start(out=ct[:], in_=class_token.broadcast_to([32, HID]))
        p0 = keep.tile([32, HID], BF16, name="p0")
        nc.scalar.dma_start(out=p0[:], in_=pos_embed[0:1, :].broadcast_to([32, HID]))
        cls = keep.tile([32, HID], F32, name="cls")
        nc.gpsimd.tensor_tensor(out=cls[:], in0=ct[:], in1=p0[:], op=MULT)

        wraw = [keep.tile([P, 4, 1024], BF16, name="wraw%d" % i) for i in range(3)]
        w_view = W.rearrange("(t p) k -> p t k", p=P)
        posq = [keep.tile([P, 8 * HID], BF16, name="posq%d" % qt) for qt in range(2)]
        pos_view = pos_embed[1:65, :].rearrange("(t l g) h -> l t (g h)", t=2, l=4, g=8)

        xc = [keep.tile([P, 1024], U32, name="xc%d" % s, align_bytes=64) for s in range(NCHUNK)]
        xs = [keep.tile([P, 1024], U8, name="xs%d" % s, align_bytes=64) for s in range(NCHUNK)]
        wc = [keep.tile([P, HID], U32, name="wc%d" % g, align_bytes=64) for g in range(NG)]
        ws = [keep.tile([P, HID], U8, name="ws%d" % g, align_bytes=64) for g in range(NG)]

        raws = {}
        rgs = {}

        def load_w(i):
            nc.sync.dma_start(out=wraw[i][:], in_=w_view[:, :, i * 1024:(i + 1) * 1024])

        def load_x(s):
            qt, g = divmod(s, NG)
            c, a = divmod(g, 2)
            raw = rawp.tile([P, 4096], BF16, name="raw%d" % s, tag="raw")
            for l in range(4):
                y0 = (qt * 4 + l) * 32 + a * 16
                nc.sync.dma_start(out=raw[l:P:4, :], in_=X[:, c, y0:y0 + 16, :].rearrange("b y x -> b (y x)"))
            raws[s] = raw

        def load_pos(qt):
            for l in range(4):
                nc.sync.dma_start(out=posq[qt][l:P:4, :], in_=pos_view[l, qt:qt + 1, :].broadcast_to([32, 8 * HID]))

        def regroup(s):
            nv = 8 if s < NG else 4
            rg = work.tile([P, 4096], BF16, name="rg%d" % s, tag="rg")
            nc.vector.tensor_copy(
                out=rg[:].bitcast(F32).rearrange("p (g y w) -> p g y w", g=8, w=16)[:, 0:nv, :, :],
                in_=raws[s][:].bitcast(F32).rearrange("p (y g w) -> p g y w", g=8, w=16)[:, 0:nv, :, :],
            )
            if nv < 8:
                nc.scalar.copy(
                    out=rg[:].bitcast(F32).rearrange("p (g y w) -> p g y w", g=8, w=16)[:, nv:8, :, :],
                    in_=raws[s][:].bitcast(F32).rearrange("p (y g w) -> p g y w", g=8, w=16)[:, nv:8, :, :],
                )
            rgs[s] = rg

        state = {"rot": 0, "n": 0, "e1": 0, "e2": 0}

        def t_bank():
            i = 4 + state["rot"]
            state["rot"] = (state["rot"] + 1) % 4
            state["n"] += 1
            return psum.tile([P, 4, P], F32, name="tp%d" % state["n"], tag="bk%d" % i)

        wgrs = {}

        def transpose_w(g):
            wgr = work.tile([P, 2048], BF16, name="wgr%d" % g, tag="wgr", align_bytes=64)
            wgrf = wgr[:].bitcast(F32).rearrange("p (t h u) -> p t h u", t=4, u=2)
            for j in range(2):
                bank = t_bank()
                for tl in range(2):
                    src = wraw[g // 2][:, 2 * j + tl, :].bitcast(F32)
                    for u in range(2):
                        k0 = (g % 2) * 256 + u * 128
                        nc.tensor.transpose(out=bank[:, 2 * tl + u, :], in_=src[:, k0:k0 + 128], identity=ident[:])
                nc.scalar.copy(out=wgrf[:, 2 * j:2 * j + 2, :, :], in_=bank[:].rearrange("p (t u) h -> p t h u", u=2))
            wgrs[g] = wgr

        grs = {}

        def transpose_x(s, hf):
            if hf == 0:
                grs[s] = work.tile([P, 4096], BF16, name="gr%d" % s, tag="gr", align_bytes=64)
            grf = grs[s][:].bitcast(F32).rearrange("p (g q u) -> p g q u", g=8, u=2)
            rgf = rgs[s][:].bitcast(F32)
            for j in range(2):
                bank = t_bank()
                g0 = 4 * hf + 2 * j
                for gl in range(2):
                    for u in range(2):
                        k0 = (g0 + gl) * 256 + u * 128
                        nc.tensor.transpose(out=bank[:, 2 * gl + u, :], in_=rgf[:, k0:k0 + 128], identity=ident[:])
                nc.scalar.copy(out=grf[:, g0:g0 + 2, :, :], in_=bank[:].rearrange("p (g u) q -> p g q u", u=2))

        def quant_w(g):
            nc.vector.quantize_mx(out=wc[g][:].bitcast(FP8X4), scales=ws[g][:], in_=wgrs[g][:])

        def quant_x(s, hf):
            nc.vector.quantize_mx(
                out=xc[s][:, hf * 512:(hf + 1) * 512].bitcast(FP8X4),
                scales=xs[s][:, hf * 512:(hf + 1) * 512],
                in_=grs[s][:, hf * 2048:(hf + 1) * 2048],
            )

        accs = {}
        closed = []

        def mx_pass(qt, gx, g, bank):
            if g == 0:
                accs[(qt, gx)] = psum.tile([P, HID], F32, name="acc%d_%d" % (qt, gx), tag="bk%d" % bank)
            s = qt * NG + g
            nc.tensor.matmul_mx(
                out=accs[(qt, gx)][:],
                lhsT=xc[s][:, gx * P:(gx + 1) * P].bitcast(FP8X4),
                lhsT_scale=xs[s][:, gx * P:(gx + 1) * P],
                rhs=wc[g][:].bitcast(FP8X4),
                rhs_scale=ws[g][:],
                start=(g == 0),
                stop=(g == NG - 1),
            )
            if g == NG - 1:
                closed.append((qt, gx))

        osts = {}
        tmps = {}

        def add_bias():
            for qt, gx in closed[state["e1"]:]:
                tmp = outp.tile([P, HID], F32, name="tmp%d_%d" % (qt, gx), tag="tmp", bufs=6)
                nc.vector.tensor_tensor(out=tmp[:], in0=accs[(qt, gx)][:], in1=bias[:], op=ADD)
                tmps[(qt, gx)] = tmp
            state["e1"] = len(closed)

        def times_pos():
            for qt, gx in closed[state["e2"]:]:
                if gx % 2 == 0:
                    osts[(qt, gx // 2)] = outp.tile([P, 2, HID], F32, name="ost%d_%d" % (qt, gx // 2), tag="ost")
                ost = osts[(qt, gx // 2)]
                on_pool = (qt == 0 and gx < 4) or (qt == 1 and gx % 2 == 0)
                eng = nc.gpsimd if on_pool else nc.vector
                eng.tensor_tensor(out=ost[:, gx % 2, :], in0=tmps[(qt, gx)][:], in1=posq[qt][:, gx * HID:(gx + 1) * HID], op=MULT)
                if gx % 2 == 1:
                    for l in range(4):
                        r0 = 1 + (qt * 4 + l) * 8 + gx - 1
                        nc.sync.dma_start(
                            out=out[:, r0:r0 + 2, :].rearrange("b g h -> b (g h)"),
                            in_=ost[l:P:4, :, :].rearrange("p g h -> p (g h)"),
                        )
            state["e2"] = len(closed)

        def early(s):
            qt, g = divmod(s, NG)
            for gx in range(4):
                mx_pass(qt, gx, g, gx)

        def whole_group(qt, gx, bank):
            for g in range(NG):
                mx_pass(qt, gx, g, bank)

        load_x(0)
        load_w(0)
        load_x(1)
        load_x(2)
        load_w(1)
        load_x(3)
        load_x(4)
        load_w(2)
        regroup(0)

        for t in range(NCHUNK):
            if t < NG:
                transpose_x(t, 0)
                transpose_w(t)
                if t >= 1:
                    early(t - 1)
                transpose_x(t, 1)
            else:
                first = 4 + state["rot"]
                transpose_x(t, 0)
                transpose_x(t, 1)
                if t < NG + 4:
                    whole_group(0, t - 2, first)
                    state["rot"] = (state["rot"] + 1) % 4
                early(t - 1)
            if t + 1 < NCHUNK:
                regroup(t + 1)
            if t + 5 < NCHUNK:
                load_x(t + 5)
            if t == 2:
                load_pos(0)
            if t == 6:
                load_pos(1)
            if t < NG:
                quant_w(t)
            quant_x(t, 0)
            quant_x(t, 1)
            add_bias()
            times_pos()

        nc.sync.dma_start(out=out[:, 0, :], in_=cls[:])
        early(NCHUNK - 1)
        add_bias()
        times_pos()
        for i in range(4):
            whole_group(1, 4 + i, 4 + (state["rot"] + i) % 4)
            add_bias()
            times_pos()
